import numpy as np
import ml_dtypes


def mxq(x, axis, fmt="e4m3"):
    dtype, down = {"e4m3": (ml_dtypes.float8_e4m3fn, 7), "e5m2": (ml_dtypes.float8_e5m2, 14)}[fmt]
    v = np.moveaxis(np.asarray(x, np.float32).astype(ml_dtypes.bfloat16).astype(np.float64), axis, -1)
    blocks = v.reshape(v.shape[:-1] + (-1, 32))
    amax = np.abs(blocks).max(-1, keepdims=True)
    byte = np.maximum(np.where(amax > 0, np.frexp(amax)[1] - 1 + 127, 0) - down, 1)
    scale = np.exp2(byte - 127.0)
    codes = (blocks / scale).astype(np.float32).astype(dtype).astype(np.float64)
    return np.moveaxis((codes * scale).reshape(v.shape), -1, axis)


WIDE = False


def mx_kscale(k):
    if not WIDE:
        return np.ones(k)
    levels = np.array([10, -10, 5, -5, 0])
    if k % 512:
        return np.exp2(np.random.permutation(np.resize(levels, k // 32))).repeat(32)
    a = np.empty((k // 512, 16))
    for p in range(k // 512):
        a[p, :8] = np.random.permutation(np.resize(levels, 8))
        for g in range(8):
            far = levels[np.abs(levels - a[p, g]) >= 10]
            a[p, g + 8] = far[np.random.randint(len(far))]
    return np.exp2(a.ravel()).repeat(32)


BF16 = ml_dtypes.bfloat16


def bf(x):
    return np.asarray(x, np.float32).astype(BF16)


def f64(x):
    return np.asarray(x).astype(np.float64)


W, M, K, N = 4, 256, 512, 256


def setup_inputs():
    s = mx_kscale(K)
    return {"x": bf(np.random.standard_normal((W, M, K)) * s),
            "weight": bf(np.random.standard_normal((W, N, K)) / np.sqrt(W * K) / s),
            "bias": bf(np.random.standard_normal((W, M, N)) / np.sqrt(W))}


def reference(x, weight, bias):
    w, m, _ = x.shape
    xq = mxq(f64(x), 2, "e4m3")
    wq = mxq(f64(weight), 2, "e4m3")
    y = (xq @ wq.transpose(0, 2, 1)).sum(0) + f64(bias).sum(0)
    m_per_rank = m // w
    return y.reshape(w, m_per_rank, -1)

@@ -1,0 +1,150 @@
+from contextlib import ExitStack
+
+import concourse.mybir as mybir
+from concourse.masks import make_identity
+
+BF16 = mybir.dt.bfloat16
+F32 = mybir.dt.float32
+U32 = mybir.dt.uint32
+U8 = mybir.dt.uint8
+FP8X4 = mybir.dt.float8_e4m3fn_x4
+ADD = mybir.AluOpType.add
+
+P = 128
+RANKS = 4
+M = 256
+N = 256
+K = 512
+PARITIES = 2
+PACK = 4
+PLANES = 2
+ROW_WORDS = K // 2
+BANKS = 8
+BIAS_AFTER_RANK = 1
+
+FLOPS = 2 * M * N * K * RANKS
+
+
+def flip(nc, psum, tag, identity, words, grouped):
+    rows = words.shape[1] // ROW_WORDS
+    flipped = psum.tile([P, rows, PLANES, P], F32, tag=tag)
+    for g in range(rows):
+        for u in range(PLANES):
+            plane = words[:, g * ROW_WORDS + u : (g + 1) * ROW_WORDS : PLANES]
+            nc.tensor.transpose(flipped[:, g, u, :], plane, identity[:])
+    nc.scalar.copy(
+        out=grouped[:].bitcast(F32).rearrange("p (g c u) -> p g c u", g=rows, u=PLANES),
+        in_=flipped[:].rearrange("p g u c -> p g c u"),
+    )
+
+
+def tile_gemmrstritonpcie_s_kernel(tc, x, weight, bias, out):
+    nc = tc.nc
+    with ExitStack() as ctx:
+        ctx.enter_context(tc.manual_schedule())
+        keep = ctx.enter_context(tc.tile_pool(name="keep", bufs=1))
+        psum = ctx.enter_context(tc.psum_pool(name="psum", bufs=BANKS - PARITIES))
+        sums = ctx.enter_context(tc.psum_pool(name="sums", bufs=1))
+
+        def x_pieces(r):
+            if r == RANKS - 1:
+                return [(s, s + 1) for s in range(PARITIES)]
+            return [(0, PARITIES)]
+
+        w_rows = []
+        x_rows = []
+        bias_rows = keep.tile([P, RANKS, PARITIES * N], BF16)
+        for r in range(RANKS):
+            w_rows.append(keep.tile([P, PARITIES * K], BF16, name="w_rows%d" % r))
+            x_rows.append(keep.tile([P, PARITIES * K], BF16, name="x_rows%d" % r))
+            nc.sync.dma_start(
+                out=w_rows[r][:], in_=weight[r].rearrange("(p s) k -> p (s k)", s=PARITIES)
+            )
+            for first, end in x_pieces(r):
+                nc.sync.dma_start(
+                    out=x_rows[r][:].rearrange("p (s k) -> p s k", s=PARITIES)[:, first:end, :],
+                    in_=x[r].rearrange("(p s) k -> p s k", s=PARITIES)[:, first:end, :],
+                )
+            if r == BIAS_AFTER_RANK:
+                nc.sync.dma_start(
+                    out=bias_rows[:], in_=bias.rearrange("r (p s) n -> p r (s n)", s=PARITIES)
+                )
+
+        identity = keep.tile([P, P], F32)
+        make_identity(nc, identity[:])
+
+        acc = [sums.tile([P, N], F32, name="acc%d" % s) for s in range(PARITIES)]
+        w_codes = [keep.tile([P, N], U32, name="w_codes%d" % r, align_bytes=64) for r in range(RANKS)]
+        w_scales = [keep.tile([P, N], U8, name="w_scales%d" % r, align_bytes=64) for r in range(RANKS)]
+        x_codes = [keep.tile([P, M], U32, name="x_codes%d" % r, align_bytes=64) for r in range(RANKS)]
+        x_scales = [keep.tile([P, M], U8, name="x_scales%d" % r, align_bytes=64) for r in range(RANKS)]
+
+        def quantise_rank(r):
+            w_grouped = keep.tile([P, N * PACK], BF16, name="w_grouped%d" % r, align_bytes=64)
+            flip(nc, psum, "flipped", identity, w_rows[r][:].bitcast(F32), w_grouped)
+            x_grouped = []
+            for first, end in x_pieces(r):
+                x_grouped.append(
+                    keep.tile(
+                        [P, (end - first) * P * PACK],
+                        BF16,
+                        name="x_grouped%d_%d" % (r, first),
+                        align_bytes=64,
+                    )
+                )
+                words = x_rows[r][:].bitcast(F32)[:, first * ROW_WORDS : end * ROW_WORDS]
+                flip(nc, psum, "flipped", identity, words, x_grouped[-1])
+
+            nc.vector.quantize_mx(
+                out=w_codes[r][:].bitcast(FP8X4), scales=w_scales[r][:], in_=w_grouped[:]
+            )
+            for (first, end), grouped in zip(x_pieces(r), x_grouped):
+                m_cols = slice(first * P, end * P)
+                nc.vector.quantize_mx(
+                    out=x_codes[r][:, m_cols].bitcast(FP8X4),
+                    scales=x_scales[r][:, m_cols],
+                    in_=grouped[:],
+                )
+
+        def multiply_rank(r):
+            for s in range(PARITIES):
+                m_cols = slice(s * P, (s + 1) * P)
+                nc.tensor.matmul_mx(
+                    out=acc[s][:],
+                    lhsT=x_codes[r][:, m_cols].bitcast(FP8X4),
+                    lhsT_scale=x_scales[r][:, m_cols],
+                    rhs=w_codes[r][:].bitcast(FP8X4),
+                    rhs_scale=w_scales[r][:],
+                    start=(r == 0),
+                    stop=(r == RANKS - 1),
+                )
+
+        bias_pairs = keep.tile([P, 2, PARITIES * N], F32)
+        bias_sum = keep.tile([P, PARITIES, N], F32)
+        for r in range(RANKS):
+            quantise_rank(r)
+            if r == BIAS_AFTER_RANK:
+                nc.vector.tensor_tensor(
+                    out=bias_pairs[:], in0=bias_rows[:, 0:2, :], in1=bias_rows[:, 2:4, :], op=ADD
+                )
+                nc.vector.tensor_tensor(
+                    out=bias_sum[:].rearrange("p s n -> p (s n)"),
+                    in0=bias_pairs[:, 0, :],
+                    in1=bias_pairs[:, 1, :],
+                    op=ADD,
+                )
+                for earlier in range(BIAS_AFTER_RANK):
+                    multiply_rank(earlier)
+        for r in range(BIAS_AFTER_RANK, RANKS):
+            multiply_rank(r)
+
+        y_rows = out.rearrange("r q n -> (r q) n").rearrange("(p s) n -> p s n", s=PARITIES)
+        for s in range(PARITIES):
+            y = keep.tile([P, N], F32, name="y%d" % s)
+            nc.vector.tensor_tensor(
+                out=y[:].rearrange("p (c t) -> p c t", t=PARITIES),
+                in0=acc[s][:].rearrange("p (t c) -> p c t", t=PARITIES),
+                in1=bias_sum[:, s, :].rearrange("p (c t) -> p c t", t=PARITIES),
+                op=ADD,
+            )
+            nc.sync.dma_start(out=y_rows[:, s, :], in_=y[:])

@@ -15,27 +15,15 @@ RANKS = 4
 M = 256
 N = 256
 K = 512
-PARITIES = 2
-PACK = 4
+S = 2
 PLANES = 2
 ROW_WORDS = K // 2
-BANKS = 8
-BIAS_AFTER_RANK = 1
 
 FLOPS = 2 * M * N * K * RANKS
 
-
-def flip(nc, psum, tag, identity, words, grouped):
-    rows = words.shape[1] // ROW_WORDS
-    flipped = psum.tile([P, rows, PLANES, P], F32, tag=tag)
-    for g in range(rows):
-        for u in range(PLANES):
-            plane = words[:, g * ROW_WORDS + u : (g + 1) * ROW_WORDS : PLANES]
-            nc.tensor.transpose(flipped[:, g, u, :], plane, identity[:])
-    nc.scalar.copy(
-        out=grouped[:].bitcast(F32).rearrange("p (g c u) -> p g c u", g=rows, u=PLANES),
-        in_=flipped[:].rearrange("p g u c -> p g c u"),
-    )
+BOTH = (0, 2)
+EVEN = (0, 1)
+ODD = (1, 2)
 
 
 def tile_gemmrstritonpcie_s_kernel(tc, x, weight, bias, out):
@@ -43,108 +31,152 @@ def tile_gemmrstritonpcie_s_kernel(tc, x, weight, bias, out):
     with ExitStack() as ctx:
         ctx.enter_context(tc.manual_schedule())
         keep = ctx.enter_context(tc.tile_pool(name="keep", bufs=1))
-        psum = ctx.enter_context(tc.psum_pool(name="psum", bufs=BANKS - PARITIES))
+        psum = ctx.enter_context(tc.psum_pool(name="psum", bufs=6))
         sums = ctx.enter_context(tc.psum_pool(name="sums", bufs=1))
 
-        def x_pieces(r):
-            if r == RANKS - 1:
-                return [(s, s + 1) for s in range(PARITIES)]
-            return [(0, PARITIES)]
+        source = {"x": x, "w": weight}
+        rows = {}
+        flipped = {}
+        grouped = {}
+        codes = {}
+        scales = {}
+        for a in ("w", "x"):
+            for r in range(RANKS):
+                rows[a, r] = keep.tile([P, S * K], BF16, name="%s_rows%d" % (a, r))
+                codes[a, r] = keep.tile([P, S * P], U32, name="%s_codes%d" % (a, r), align_bytes=64)
+                scales[a, r] = keep.tile([P, S * P], U8, name="%s_scales%d" % (a, r), align_bytes=64)
+                grouped[a, r] = keep.tile([P, S * K], BF16, name="%s_grouped%d" % (a, r), align_bytes=64)
 
-        w_rows = []
-        x_rows = []
-        bias_rows = keep.tile([P, RANKS, PARITIES * N], BF16)
-        for r in range(RANKS):
-            w_rows.append(keep.tile([P, PARITIES * K], BF16, name="w_rows%d" % r))
-            x_rows.append(keep.tile([P, PARITIES * K], BF16, name="x_rows%d" % r))
+        def load(a, r, part=BOTH):
+            f, e = part
             nc.sync.dma_start(
-                out=w_rows[r][:], in_=weight[r].rearrange("(p s) k -> p (s k)", s=PARITIES)
+                out=rows[a, r][:].rearrange("p (s k) -> p s k", s=S)[:, f:e, :],
+                in_=source[a][r].rearrange("(p s) k -> p s k", s=S)[:, f:e, :],
             )
-            for first, end in x_pieces(r):
-                nc.sync.dma_start(
-                    out=x_rows[r][:].rearrange("p (s k) -> p s k", s=PARITIES)[:, first:end, :],
-                    in_=x[r].rearrange("(p s) k -> p s k", s=PARITIES)[:, first:end, :],
-                )
-            if r == BIAS_AFTER_RANK:
-                nc.sync.dma_start(
-                    out=bias_rows[:], in_=bias.rearrange("r (p s) n -> p r (s n)", s=PARITIES)
-                )
+
+        bias_rows = keep.tile([P, RANKS, S * N], BF16)
+
+        def load_bias(f, e):
+            nc.sync.dma_start(
+                out=bias_rows[:, f:e, :], in_=bias[f:e].rearrange("r (p s) n -> p r (s n)", s=S)
+            )
 
         identity = keep.tile([P, P], F32)
+
+        def flip(a, r, part=BOTH):
+            f, e = part
+            words = rows[a, r][:].bitcast(F32)
+            t = psum.tile([P, e - f, PLANES, P], F32, name="flipped_%s%d_%d" % (a, r, f), tag="flipped")
+            flipped[a, r, f] = t
+            for s in range(f, e):
+                for u in range(PLANES):
+                    nc.tensor.transpose(
+                        t[:, s - f, u, :], words[:, s * ROW_WORDS + u : (s + 1) * ROW_WORDS : PLANES], identity[:]
+                    )
+
+        def group(engine, a, r, part=BOTH):
+            f, e = part
+            out_ = grouped[a, r][:].bitcast(F32)[:, f * ROW_WORDS : e * ROW_WORDS]
+            out_ = out_.rearrange("p (g c u) -> p g c u", g=e - f, u=PLANES)
+            in_ = flipped[a, r, f][:].rearrange("p g u c -> p g c u")
+            if engine == "act":
+                nc.scalar.copy(out=out_, in_=in_)
+            else:
+                nc.vector.tensor_copy(out=out_, in_=in_)
+
+        def quantise(a, r, part=BOTH):
+            f, e = part
+            cols = slice(f * P, e * P)
+            nc.vector.quantize_mx(
+                out=codes[a, r][:, cols].bitcast(FP8X4),
+                scales=scales[a, r][:, cols],
+                in_=grouped[a, r][:, f * K : e * K],
+            )
+
+        acc = [sums.tile([P, N], F32, name="acc%d" % s) for s in range(S)]
+
+        def multiply(r, s):
+            m_cols = slice(s * P, (s + 1) * P)
+            nc.tensor.matmul_mx(
+                out=acc[s][:],
+                lhsT=codes["x", r][:, m_cols].bitcast(FP8X4),
+                lhsT_scale=scales["x", r][:, m_cols],
+                rhs=codes["w", r][:].bitcast(FP8X4),
+                rhs_scale=scales["w", r][:],
+                start=(r == 0),
+                stop=(r == RANKS - 1),
+            )
+
+        def add(out_, in0, in1):
+            nc.vector.tensor_tensor(out=out_, in0=in0, in1=in1, op=ADD)
+
+        y_rows = out.rearrange("r q n -> (r q) n").rearrange("(p s) n -> p s n", s=S)
+        bias_sum = keep.tile([P, S, N], F32)
+        y = [keep.tile([P, N], F32, name="y%d" % s) for s in range(S)]
+
+        def finish(s, queue):
+            add(
+                y[s][:].rearrange("p (c t) -> p c t", t=S),
+                acc[s][:].rearrange("p (t c) -> p c t", t=S),
+                bias_sum[:, s, :].rearrange("p (c t) -> p c t", t=S),
+            )
+            queue.dma_start(out=y_rows[:, s, :], in_=y[s][:])
+
+        HALVES = (EVEN, ODD)
+        for part in HALVES:
+            load("w", 0, part)
+        for part in HALVES:
+            load("x", 0, part)
+        load("w", 1)
+        load_bias(0, 2)
+        load("x", 1)
+        load("w", 2)
+        load("x", 2)
+        load_bias(2, 4)
+        for part in HALVES:
+            load("w", 3, part)
+        for part in HALVES:
+            load("x", 3, part)
         make_identity(nc, identity[:])
 
-        acc = [sums.tile([P, N], F32, name="acc%d" % s) for s in range(PARITIES)]
-        w_codes = [keep.tile([P, N], U32, name="w_codes%d" % r, align_bytes=64) for r in range(RANKS)]
-        w_scales = [keep.tile([P, N], U8, name="w_scales%d" % r, align_bytes=64) for r in range(RANKS)]
-        x_codes = [keep.tile([P, M], U32, name="x_codes%d" % r, align_bytes=64) for r in range(RANKS)]
-        x_scales = [keep.tile([P, M], U8, name="x_scales%d" % r, align_bytes=64) for r in range(RANKS)]
+        pair01 = keep.tile([P, S * N], F32)
+        pair23 = keep.tile([P, S * N], F32)
 
-        def quantise_rank(r):
-            w_grouped = keep.tile([P, N * PACK], BF16, name="w_grouped%d" % r, align_bytes=64)
-            flip(nc, psum, "flipped", identity, w_rows[r][:].bitcast(F32), w_grouped)
-            x_grouped = []
-            for first, end in x_pieces(r):
-                x_grouped.append(
-                    keep.tile(
-                        [P, (end - first) * P * PACK],
-                        BF16,
-                        name="x_grouped%d_%d" % (r, first),
-                        align_bytes=64,
-                    )
-                )
-                words = x_rows[r][:].bitcast(F32)[:, first * ROW_WORDS : end * ROW_WORDS]
-                flip(nc, psum, "flipped", identity, words, x_grouped[-1])
+        def bring(a, r):
+            for part in HALVES:
+                flip(a, r, part)
+                group("act", a, r, part)
 
-            nc.vector.quantize_mx(
-                out=w_codes[r][:].bitcast(FP8X4), scales=w_scales[r][:], in_=w_grouped[:]
-            )
-            for (first, end), grouped in zip(x_pieces(r), x_grouped):
-                m_cols = slice(first * P, end * P)
-                nc.vector.quantize_mx(
-                    out=x_codes[r][:, m_cols].bitcast(FP8X4),
-                    scales=x_scales[r][:, m_cols],
-                    in_=grouped[:],
-                )
+        def quant(a, r):
+            for part in HALVES:
+                quantise(a, r, part)
 
-        def multiply_rank(r):
-            for s in range(PARITIES):
-                m_cols = slice(s * P, (s + 1) * P)
-                nc.tensor.matmul_mx(
-                    out=acc[s][:],
-                    lhsT=x_codes[r][:, m_cols].bitcast(FP8X4),
-                    lhsT_scale=x_scales[r][:, m_cols],
-                    rhs=w_codes[r][:].bitcast(FP8X4),
-                    rhs_scale=w_scales[r][:],
-                    start=(r == 0),
-                    stop=(r == RANKS - 1),
-                )
+        def mult(r):
+            for s in range(S):
+                multiply(r, s)
 
-        bias_pairs = keep.tile([P, 2, PARITIES * N], F32)
-        bias_sum = keep.tile([P, PARITIES, N], F32)
-        for r in range(RANKS):
-            quantise_rank(r)
-            if r == BIAS_AFTER_RANK:
-                nc.vector.tensor_tensor(
-                    out=bias_pairs[:], in0=bias_rows[:, 0:2, :], in1=bias_rows[:, 2:4, :], op=ADD
-                )
-                nc.vector.tensor_tensor(
-                    out=bias_sum[:].rearrange("p s n -> p (s n)"),
-                    in0=bias_pairs[:, 0, :],
-                    in1=bias_pairs[:, 1, :],
-                    op=ADD,
-                )
-                for earlier in range(BIAS_AFTER_RANK):
-                    multiply_rank(earlier)
-        for r in range(BIAS_AFTER_RANK, RANKS):
-            multiply_rank(r)
-
-        y_rows = out.rearrange("r q n -> (r q) n").rearrange("(p s) n -> p s n", s=PARITIES)
-        for s in range(PARITIES):
-            y = keep.tile([P, N], F32, name="y%d" % s)
-            nc.vector.tensor_tensor(
-                out=y[:].rearrange("p (c t) -> p c t", t=PARITIES),
-                in0=acc[s][:].rearrange("p (t c) -> p c t", t=PARITIES),
-                in1=bias_sum[:, s, :].rearrange("p (c t) -> p c t", t=PARITIES),
-                op=ADD,
-            )
-            nc.sync.dma_start(out=y_rows[:, s, :], in_=y[:])
+        bring("w", 0)
+        quant("w", 0)
+        bring("x", 0)
+        quant("x", 0)
+        add(pair01[:], bias_rows[:, 0, :], bias_rows[:, 1, :])
+        bring("w", 1)
+        mult(0)
+        bring("x", 1)
+        quant("w", 1)
+        quant("x", 1)
+        add(pair23[:], bias_rows[:, 2, :], bias_rows[:, 3, :])
+        bring("w", 2)
+        bring("x", 2)
+        mult(1)
+        quant("w", 2)
+        add(bias_sum[:].rearrange("p s n -> p (s n)"), pair01[:], pair23[:])
+        quant("x", 2)
+        bring("w", 3)
+        bring("x", 3)
+        quant("w", 3)
+        quant("x", 3)
+        mult(2)
+        mult(3)
+        finish(0, nc.sync)
+        finish(1, nc.sync)

@@ -125,22 +125,20 @@ def tile_gemmrstritonpcie_s_kernel(tc, x, weight, bias, out):
         HALVES = (EVEN, ODD)
         for part in HALVES:
             load("w", 0, part)
-        for part in HALVES:
-            load("x", 0, part)
+        load("x", 0)
         load("w", 1)
-        load_bias(0, 2)
         load("x", 1)
+        load_bias(0, 2)
         load("w", 2)
         load("x", 2)
-        load_bias(2, 4)
-        for part in HALVES:
-            load("w", 3, part)
-        for part in HALVES:
-            load("x", 3, part)
+        load_bias(2, 3)
+        load("w", 3)
+        load("x", 3)
+        load_bias(3, 4)
         make_identity(nc, identity[:])
 
-        pair01 = keep.tile([P, S * N], F32)
-        pair23 = keep.tile([P, S * N], F32)
+        bias01 = keep.tile([P, S * N], F32)
+        bias012 = keep.tile([P, S * N], F32)
 
         def bring(a, r):
             for part in HALVES:
@@ -159,23 +157,23 @@ def tile_gemmrstritonpcie_s_kernel(tc, x, weight, bias, out):
         quant("w", 0)
         bring("x", 0)
         quant("x", 0)
-        add(pair01[:], bias_rows[:, 0, :], bias_rows[:, 1, :])
         bring("w", 1)
-        mult(0)
-        bring("x", 1)
         quant("w", 1)
+        bring("x", 1)
+        mult(0)
+        add(bias01[:], bias_rows[:, 0, :], bias_rows[:, 1, :])
         quant("x", 1)
-        add(pair23[:], bias_rows[:, 2, :], bias_rows[:, 3, :])
         bring("w", 2)
-        bring("x", 2)
-        mult(1)
         quant("w", 2)
-        add(bias_sum[:].rearrange("p s n -> p (s n)"), pair01[:], pair23[:])
+        bring("x", 2)
+        add(bias012[:], bias01[:], bias_rows[:, 2, :])
         quant("x", 2)
         bring("w", 3)
         bring("x", 3)
+        add(bias_sum[:].rearrange("p s n -> p (s n)"), bias012[:], bias_rows[:, 3, :])
         quant("w", 3)
         quant("x", 3)
+        mult(1)
         mult(2)
         mult(3)
         finish(0, nc.sync)

@@ -128,13 +128,14 @@ def tile_gemmrstritonpcie_s_kernel(tc, x, weight, bias, out):
         load("x", 0)
         load("w", 1)
         load("x", 1)
-        load_bias(0, 2)
         load("w", 2)
+        load_bias(0, 2)
         load("x", 2)
         load_bias(2, 3)
         load("w", 3)
-        load("x", 3)
         load_bias(3, 4)
+        for part in HALVES:
+            load("x", 3, part)
         make_identity(nc, identity[:])
 
         bias01 = keep.tile([P, S * N], F32)
@@ -158,19 +159,19 @@ def tile_gemmrstritonpcie_s_kernel(tc, x, weight, bias, out):
         bring("x", 0)
         quant("x", 0)
         bring("w", 1)
-        quant("w", 1)
         bring("x", 1)
-        mult(0)
+        quant("w", 1)
         add(bias01[:], bias_rows[:, 0, :], bias_rows[:, 1, :])
         quant("x", 1)
         bring("w", 2)
-        quant("w", 2)
-        bring("x", 2)
+        mult(0)
         add(bias012[:], bias01[:], bias_rows[:, 2, :])
+        quant("w", 2)
+        add(bias_sum[:].rearrange("p s n -> p (s n)"), bias012[:], bias_rows[:, 3, :])
+        bring("x", 2)
         quant("x", 2)
         bring("w", 3)
         bring("x", 3)
-        add(bias_sum[:].rearrange("p s n -> p (s n)"), bias012[:], bias_rows[:, 3, :])
         quant("w", 3)
         quant("x", 3)
         mult(1)

@@ -31,7 +31,7 @@ def tile_gemmrstritonpcie_s_kernel(tc, x, weight, bias, out):
     with ExitStack() as ctx:
         ctx.enter_context(tc.manual_schedule())
         keep = ctx.enter_context(tc.tile_pool(name="keep", bufs=1))
-        psum = ctx.enter_context(tc.psum_pool(name="psum", bufs=6))
+        psum = ctx.enter_context(tc.psum_pool(name="psum", bufs=5))
         sums = ctx.enter_context(tc.psum_pool(name="sums", bufs=1))
 
         source = {"x": x, "w": weight}
@@ -138,6 +138,15 @@ def tile_gemmrstritonpcie_s_kernel(tc, x, weight, bias, out):
             load("x", 3, part)
         make_identity(nc, identity[:])
 
+        zeros = keep.tile([P, P], F32)
+        nc.vector.memset(zeros[:], 0.0)
+        unread = sums.tile([P, P], F32, name="unread")
+
+        def warm(count):
+            for i in range(count):
+                nc.tensor.matmul(unread[:], lhsT=zeros[:], rhs=zeros[:], start=True, stop=True)
+
+
         bias01 = keep.tile([P, S * N], F32)
         bias012 = keep.tile([P, S * N], F32)
 
@@ -154,11 +163,13 @@ def tile_gemmrstritonpcie_s_kernel(tc, x, weight, bias, out):
             for s in range(S):
                 multiply(r, s)
 
+        warm(3)
         bring("w", 0)
         quant("w", 0)
         bring("x", 0)
         quant("x", 0)
         bring("w", 1)
+        warm(1)
         bring("x", 1)
         quant("w", 1)
         add(bias01[:], bias_rows[:, 0, :], bias_rows[:, 1, :])
@@ -170,6 +181,7 @@ def tile_gemmrstritonpcie_s_kernel(tc, x, weight, bias, out):
         add(bias_sum[:].rearrange("p s n -> p (s n)"), bias012[:], bias_rows[:, 3, :])
         bring("x", 2)
         quant("x", 2)
+        warm(1)
         bring("w", 3)
         bring("x", 3)
         quant("w", 3)

@@ -133,9 +133,9 @@ def tile_gemmrstritonpcie_s_kernel(tc, x, weight, bias, out):
         load("x", 2)
         load_bias(2, 3)
         load("w", 3)
+        load("x", 3, EVEN)
         load_bias(3, 4)
-        for part in HALVES:
-            load("x", 3, part)
+        load("x", 3, ODD)
         make_identity(nc, identity[:])
 
         zeros = keep.tile([P, P], F32)
@@ -166,7 +166,10 @@ def tile_gemmrstritonpcie_s_kernel(tc, x, weight, bias, out):
         warm(3)
         bring("w", 0)
         quant("w", 0)
-        bring("x", 0)
+        flip("x", 0, EVEN)
+        group("act", "x", 0, EVEN)
+        flip("x", 0, ODD)
+        group("dve", "x", 0, ODD)
         quant("x", 0)
         bring("w", 1)
         warm(1)
@@ -178,9 +181,9 @@ def tile_gemmrstritonpcie_s_kernel(tc, x, weight, bias, out):
         mult(0)
         add(bias012[:], bias01[:], bias_rows[:, 2, :])
         quant("w", 2)
-        add(bias_sum[:].rearrange("p s n -> p (s n)"), bias012[:], bias_rows[:, 3, :])
         bring("x", 2)
         quant("x", 2)
+        add(bias_sum[:].rearrange("p s n -> p (s n)"), bias012[:], bias_rows[:, 3, :])
         warm(1)
         bring("w", 3)
         bring("x", 3)

from contextlib import ExitStack

import concourse.mybir as mybir
from concourse.masks import make_identity

BF16 = mybir.dt.bfloat16
F32 = mybir.dt.float32
U32 = mybir.dt.uint32
U8 = mybir.dt.uint8
FP8X4 = mybir.dt.float8_e4m3fn_x4
ADD = mybir.AluOpType.add

P = 128
RANKS = 4
M = 256
N = 256
K = 512
S = 2
PLANES = 2
ROW_WORDS = K // 2

FLOPS = 2 * M * N * K * RANKS

BOTH = (0, 2)
EVEN = (0, 1)
ODD = (1, 2)


def tile_gemmrstritonpcie_s_kernel(tc, x, weight, bias, out):
    nc = tc.nc
    with ExitStack() as ctx:
        ctx.enter_context(tc.manual_schedule())
        keep = ctx.enter_context(tc.tile_pool(name="keep", bufs=1))
        psum = ctx.enter_context(tc.psum_pool(name="psum", bufs=5))
        sums = ctx.enter_context(tc.psum_pool(name="sums", bufs=1))

        source = {"x": x, "w": weight}
        rows = {}
        flipped = {}
        grouped = {}
        codes = {}
        scales = {}
        for a in ("w", "x"):
            for r in range(RANKS):
                rows[a, r] = keep.tile([P, S * K], BF16, name="%s_rows%d" % (a, r))
                codes[a, r] = keep.tile([P, S * P], U32, name="%s_codes%d" % (a, r), align_bytes=64)
                scales[a, r] = keep.tile([P, S * P], U8, name="%s_scales%d" % (a, r), align_bytes=64)
                grouped[a, r] = keep.tile([P, S * K], BF16, name="%s_grouped%d" % (a, r), align_bytes=64)

        def load(a, r, part=BOTH):
            f, e = part
            nc.sync.dma_start(
                out=rows[a, r][:].rearrange("p (s k) -> p s k", s=S)[:, f:e, :],
                in_=source[a][r].rearrange("(p s) k -> p s k", s=S)[:, f:e, :],
            )

        bias_rows = keep.tile([P, RANKS, S * N], BF16)

        def load_bias(f, e):
            nc.sync.dma_start(
                out=bias_rows[:, f:e, :], in_=bias[f:e].rearrange("r (p s) n -> p r (s n)", s=S)
            )

        identity = keep.tile([P, P], F32)

        def flip(a, r, part=BOTH):
            f, e = part
            words = rows[a, r][:].bitcast(F32)
            t = psum.tile([P, e - f, PLANES, P], F32, name="flipped_%s%d_%d" % (a, r, f), tag="flipped")
            flipped[a, r, f] = t
            for s in range(f, e):
                for u in range(PLANES):
                    nc.tensor.transpose(
                        t[:, s - f, u, :], words[:, s * ROW_WORDS + u : (s + 1) * ROW_WORDS : PLANES], identity[:]
                    )

        def group(engine, a, r, part=BOTH):
            f, e = part
            out_ = grouped[a, r][:].bitcast(F32)[:, f * ROW_WORDS : e * ROW_WORDS]
            out_ = out_.rearrange("p (g c u) -> p g c u", g=e - f, u=PLANES)
            in_ = flipped[a, r, f][:].rearrange("p g u c -> p g c u")
            if engine == "act":
                nc.scalar.copy(out=out_, in_=in_)
            else:
                nc.vector.tensor_copy(out=out_, in_=in_)

        def quantise(a, r, part=BOTH):
            f, e = part
            cols = slice(f * P, e * P)
            nc.vector.quantize_mx(
                out=codes[a, r][:, cols].bitcast(FP8X4),
                scales=scales[a, r][:, cols],
                in_=grouped[a, r][:, f * K : e * K],
            )

        acc = [sums.tile([P, N], F32, name="acc%d" % s) for s in range(S)]

        def multiply(r, s):
            m_cols = slice(s * P, (s + 1) * P)
            nc.tensor.matmul_mx(
                out=acc[s][:],
                lhsT=codes["x", r][:, m_cols].bitcast(FP8X4),
                lhsT_scale=scales["x", r][:, m_cols],
                rhs=codes["w", r][:].bitcast(FP8X4),
                rhs_scale=scales["w", r][:],
                start=(r == 0),
                stop=(r == RANKS - 1),
            )

        def add(out_, in0, in1):
            nc.vector.tensor_tensor(out=out_, in0=in0, in1=in1, op=ADD)

        y_rows = out.rearrange("r q n -> (r q) n").rearrange("(p s) n -> p s n", s=S)
        bias_sum = keep.tile([P, S, N], F32)
        y = [keep.tile([P, N], F32, name="y%d" % s) for s in range(S)]

        def finish(s, queue):
            add(
                y[s][:].rearrange("p (c t) -> p c t", t=S),
                acc[s][:].rearrange("p (t c) -> p c t", t=S),
                bias_sum[:, s, :].rearrange("p (c t) -> p c t", t=S),
            )
            queue.dma_start(out=y_rows[:, s, :], in_=y[s][:])

        HALVES = (EVEN, ODD)
        for part in HALVES:
            load("w", 0, part)
        load("x", 0)
        load("w", 1)
        load("x", 1)
        load("w", 2)
        load_bias(0, 2)
        load("x", 2)
        load_bias(2, 3)
        load("w", 3)
        load("x", 3, EVEN)
        load_bias(3, 4)
        load("x", 3, ODD)
        make_identity(nc, identity[:])

        zeros = keep.tile([P, P], F32)
        nc.vector.memset(zeros[:], 0.0)
        unread = sums.tile([P, P], F32, name="unread")

        def warm(count):
            for i in range(count):
                nc.tensor.matmul(unread[:], lhsT=zeros[:], rhs=zeros[:], start=True, stop=True)


        bias01 = keep.tile([P, S * N], F32)
        bias012 = keep.tile([P, S * N], F32)

        def bring(a, r):
            for part in HALVES:
                flip(a, r, part)
                group("act", a, r, part)

        def quant(a, r):
            for part in HALVES:
                quantise(a, r, part)

        def mult(r):
            for s in range(S):
                multiply(r, s)

        warm(3)
        bring("w", 0)
        quant("w", 0)
        flip("x", 0, EVEN)
        group("act", "x", 0, EVEN)
        flip("x", 0, ODD)
        group("dve", "x", 0, ODD)
        quant("x", 0)
        bring("w", 1)
        warm(1)
        bring("x", 1)
        quant("w", 1)
        add(bias01[:], bias_rows[:, 0, :], bias_rows[:, 1, :])
        quant("x", 1)
        bring("w", 2)
        mult(0)
        add(bias012[:], bias01[:], bias_rows[:, 2, :])
        quant("w", 2)
        bring("x", 2)
        quant("x", 2)
        add(bias_sum[:].rearrange("p s n -> p (s n)"), bias012[:], bias_rows[:, 3, :])
        warm(1)
        bring("w", 3)
        bring("x", 3)
        quant("w", 3)
        quant("x", 3)
        mult(1)
        mult(2)
        mult(3)
        finish(0, nc.sync)
        finish(1, nc.sync)
